import numpy as np
import ml_dtypes


def mxq(x, axis, fmt="e4m3"):
    dtype, down = {"e4m3": (ml_dtypes.float8_e4m3fn, 7), "e5m2": (ml_dtypes.float8_e5m2, 14)}[fmt]
    v = np.moveaxis(np.asarray(x, np.float32).astype(ml_dtypes.bfloat16).astype(np.float64), axis, -1)
    blocks = v.reshape(v.shape[:-1] + (-1, 32))
    amax = np.abs(blocks).max(-1, keepdims=True)
    byte = np.maximum(np.where(amax > 0, np.frexp(amax)[1] - 1 + 127, 0) - down, 1)
    scale = np.exp2(byte - 127.0)
    codes = (blocks / scale).astype(np.float32).astype(dtype).astype(np.float64)
    return np.moveaxis((codes * scale).reshape(v.shape), -1, axis)


WIDE = False


def mx_kscale(k):
    if not WIDE:
        return np.ones(k)
    levels = np.array([10, -10, 5, -5, 0])
    a = np.random.permutation(np.resize(levels, k // 512 * 4)).reshape(k // 512, 4)
    idx = np.arange(k)
    return np.exp2(a[idx // 512, idx % 128 // 32])


BF16 = ml_dtypes.bfloat16


def bf(x):
    return np.asarray(x, np.float32).astype(BF16)


def f64(x):
    return np.asarray(x).astype(np.float64)


B, S, H, NH = 16, 256, 512, 16
LN_EPS = 1e-5


def silu(v):
    return v / (1.0 + np.exp(-v))


def setup_inputs():
    s, t = mx_kscale(H), mx_kscale(H)
    w = 1.0 / np.sqrt(H)
    z = (np.random.standard_normal((B, S, H)) + 0.3 * np.random.standard_normal((B, S, 1))) * 2.0 / S
    return {"z": bf(z),
            "hidden_states": bf(np.random.standard_normal((B, S, H)) * s),
            "Wg": bf(np.random.standard_normal((H, H)) * w / s[:, None]),
            "Wo": bf(np.random.standard_normal((H, H)) * w / t[:, None]),
            "gamma": bf((1.0 + 0.1 * np.random.standard_normal(H)) * t),
            "beta": bf(0.1 * np.random.standard_normal(H) * t)}


def reference(z, hidden_states, Wg, Wo, gamma, beta):
    z = f64(z)
    g = mxq(f64(hidden_states), 2, "e4m3") @ mxq(f64(Wg), 0, "e4m3")
    mu = np.mean(z, axis=-1, keepdims=True)
    var = np.mean(np.square(z - mu), axis=-1, keepdims=True)
    zn = (z - mu) * (1.0 / np.sqrt(var + LN_EPS)) * f64(gamma) + f64(beta)
    h = zn * silu(g)
    return mxq(h, 2, "e4m3") @ mxq(f64(Wo), 0, "e4m3")

@@ -1,0 +1,284 @@
+from contextlib import ExitStack
+
+import concourse.mybir as mybir
+from concourse.masks import make_identity
+
+F32 = mybir.dt.float32
+BF16 = mybir.dt.bfloat16
+U32 = mybir.dt.uint32
+U8 = mybir.dt.uint8
+FP8X4 = mybir.dt.float8_e4m3fn_x4
+ALU = mybir.AluOpType
+ACT = mybir.ActivationFunctionType
+
+P = 128
+PACK = 4
+H = 512
+TOKENS = 16 * 256
+TILES = 2
+CHUNK = TILES * P
+N_CHUNKS = TOKENS // CHUNK
+GROUPS = H // P
+HALVES = 2
+LN_EPS = 1e-5
+STORE_BUFS = 6
+
+FLOPS = 2 * 2 * TOKENS * H * H
+
+
+def tile_gatedlinearattention_pb_t_kernel(tc, z, hidden_states, Wg, Wo, gamma, beta, out):
+    nc = tc.nc
+
+    z_chunks = z.flatten_outer_dims().rearrange("(c p r) f -> c p (r f)", p=P, r=TILES)
+    hs_chunks = hidden_states.flatten_outer_dims().rearrange("(c p r) f -> c p (r f)", p=P, r=TILES)
+    out_chunks = out.flatten_outer_dims().rearrange("(c p r) f -> c p (r f)", p=P, r=TILES)
+
+    with ExitStack() as stack:
+        const = stack.enter_context(tc.tile_pool(name="const", bufs=1))
+        inputs = stack.enter_context(tc.tile_pool(name="inputs", bufs=N_CHUNKS))
+        work = stack.enter_context(tc.tile_pool(name="work", bufs=3))
+        stats = stack.enter_context(tc.tile_pool(name="stats", bufs=5))
+        stores = stack.enter_context(tc.tile_pool(name="stores", bufs=STORE_BUFS))
+        psum = stack.enter_context(tc.psum_pool(name="psum", bufs=2))
+
+        ident = const.tile([P, P], F32, name="ident")
+        make_identity(nc, ident[:])
+        minus_half = const.tile([P, TILES], F32, name="minus_half")
+        nc.gpsimd.memset(minus_half[:], -0.5)
+        table_warmer = const.tile([P, 1], F32, name="table_warmer")
+        nc.scalar.activation(out=table_warmer[:], in_=minus_half[:, 0:1], func=ACT.Silu)
+        gb_rows = const.tile([P, P], BF16, name="gb_rows")
+        nc.vector.memset(gb_rows[:], 0.0)
+
+        z_sb = {}
+        hs_sb = {}
+
+        def load_chunk(c):
+            z_sb[c] = inputs.tile([P, TILES * H], BF16, name="z_sb")
+            nc.sync.dma_start(out=z_sb[c][:], in_=z_chunks[c])
+            hs_sb[c] = inputs.tile([P, TILES * H], BF16, name="hs_sb")
+            nc.sync.dma_start(out=hs_sb[c][:], in_=hs_chunks[c])
+
+        wg_raw = const.tile([P, PACK, H], BF16, name="wg_raw")
+        wo_raw = const.tile([P, PACK, H], BF16, name="wo_raw")
+
+        load_chunk(0)
+        nc.sync.dma_start(
+            out=wg_raw[:].rearrange("q (u e) n -> q u (e n)", u=HALVES),
+            in_=Wg.rearrange("(u q e) n -> q u (e n)", u=HALVES, q=P),
+        )
+        load_chunk(1)
+        nc.sync.dma_start(out=wo_raw[:], in_=Wo.rearrange("(j p) n -> p j n", p=P))
+        nc.sync.dma_start(out=gb_rows[0:GROUPS, :], in_=gamma.rearrange("(j p) -> j p", p=P))
+        nc.sync.dma_start(out=gb_rows[GROUPS : 2 * GROUPS, :], in_=beta.rearrange("(j p) -> j p", p=P))
+        for c in range(2, N_CHUNKS):
+            load_chunk(c)
+
+        def regroup_weight(copy, raw, name):
+            grouped = const.tile([P, H, PACK], BF16, name=name, align_bytes=64)
+            copy(out=grouped[:], in_=raw[:].rearrange("p t n -> p n t"))
+            return grouped
+
+        def quantise_weight(grouped, name):
+            codes = const.tile([P, H], U32, name=name + "_codes", align_bytes=64)
+            scales = const.tile([P, H], U8, name=name + "_scales", align_bytes=64)
+            nc.vector.quantize_mx(
+                out=codes[:].bitcast(FP8X4),
+                scales=scales[:],
+                in_=grouped[:].rearrange("p n t -> p (n t)"),
+            )
+            return codes, scales
+
+        def spread_gamma_beta():
+            gb_rows_f32 = const.tile([P, P], F32, name="gb_rows_f32")
+            nc.vector.tensor_copy(out=gb_rows_f32[:], in_=gb_rows[:])
+            gb_ps = psum.tile([P, HALVES, CHUNK], F32, name="gb_ps", tag="hsT_ps")
+            nc.tensor.transpose(gb_ps[:, 0, 0:P], gb_rows_f32[:], ident[:])
+            gb = const.tile([P, 2 * GROUPS], F32, name="gb")
+            nc.vector.tensor_copy(out=gb[:], in_=gb_ps[:, 0, 0 : 2 * GROUPS])
+            return gb
+
+        mean_var = {}
+        rstd = {}
+        zc = {}
+        zcT_ps = {}
+        hsT_ps = {}
+        hs_grouped = {}
+        hs_mx = {}
+        g_ps = {}
+        gate = {}
+        zn = {}
+        h_grouped = {}
+        h_mx = {}
+        out_ps = {}
+        weights = {}
+
+        def token_statistics(c):
+            partial = stats.tile([P, TILES, 6], F32, name="partial")
+            mean_var[c] = stats.tile([P, TILES, 2], F32, name="mean_var")
+            for r in range(TILES):
+                nc.vector.bn_stats(out=partial[:, r, :], in_=z_sb[c][:, r * H : (r + 1) * H])
+            for r in range(TILES):
+                nc.vector.bn_aggr(out=mean_var[c][:, r, :], in_=partial[:, r, :])
+            var_eps = stats.tile([P, TILES], F32, name="var_eps")
+            nc.gpsimd.tensor_scalar(
+                out=var_eps[:], in0=mean_var[c][:, :, 1], scalar1=LN_EPS, scalar2=None, op0=ALU.add
+            )
+            rstd[c] = stats.tile([P, TILES], F32, name="rstd")
+            nc.gpsimd.tensor_tensor(out=rstd[c][:], in0=var_eps[:], in1=minus_half[:], op=ALU.pow)
+
+        def centre_and_scale(c, r):
+            if r == 0:
+                zc[c] = work.tile([P, TILES, H], F32, name="zc")
+            nc.vector.tensor_scalar(
+                out=zc[c][:, r, :],
+                in0=z_sb[c][:, r * H : (r + 1) * H],
+                scalar1=mean_var[c][:, r, 0:1],
+                scalar2=rstd[c][:, r : r + 1],
+                op0=ALU.subtract,
+                op1=ALU.mult,
+            )
+
+        def transpose_zc(c):
+            for pair in range(GROUPS // 2):
+                zcT_ps[c, pair] = psum.tile([P, 2, CHUNK], F32, name="zcT_ps")
+                for i in range(2):
+                    j = 2 * pair + i
+                    for r in range(TILES):
+                        nc.tensor.transpose(
+                            zcT_ps[c, pair][:, i, r * P : (r + 1) * P],
+                            zc[c][:, r, j * P : (j + 1) * P],
+                            ident[:],
+                        )
+
+        def transpose_hs(c):
+            words = hs_sb[c][:].bitcast(F32)
+            hsT_ps[c] = psum.tile([P, HALVES, CHUNK], F32, name="hsT_ps")
+            for r in range(TILES):
+                for u in range(HALVES):
+                    first = (r * HALVES + u) * P
+                    nc.tensor.transpose(
+                        hsT_ps[c][:, u, r * P : (r + 1) * P], words[:, first : first + P], ident[:]
+                    )
+
+        def regroup_hs(c):
+            hs_grouped[c] = work.tile([P, CHUNK * PACK], BF16, name="hs_grouped", align_bytes=64)
+            copy = nc.vector.tensor_copy if c % 2 == 0 else nc.scalar.copy
+            copy(
+                out=hs_grouped[c][:].bitcast(F32).rearrange("p (w u) -> p w u", u=HALVES),
+                in_=hsT_ps[c][:].rearrange("p u w -> p w u"),
+            )
+
+        def quantise(grouped, name):
+            codes = work.tile([P, CHUNK], U32, name=name + "_codes", align_bytes=64)
+            scales = work.tile([P, CHUNK], U8, name=name + "_scales", align_bytes=64)
+            nc.vector.quantize_mx(out=codes[:].bitcast(FP8X4), scales=scales[:], in_=grouped[:])
+            return codes, scales
+
+        def first_product(c):
+            wg_codes, wg_scales = weights["wg"]
+            hs_codes, hs_scales = hs_mx[c]
+            for pair in range(GROUPS // 2):
+                g_ps[c, pair] = psum.tile([P, 2, CHUNK], F32, name="g_ps")
+                for i in range(2):
+                    j = 2 * pair + i
+                    nc.tensor.matmul_mx(
+                        out=g_ps[c, pair][:, i, :],
+                        lhsT=wg_codes[:, j * P : (j + 1) * P].bitcast(FP8X4),
+                        lhsT_scale=wg_scales[:, j * P : (j + 1) * P],
+                        rhs=hs_codes[:].bitcast(FP8X4),
+                        rhs_scale=hs_scales[:],
+                        start=True,
+                        stop=True,
+                    )
+
+        def silu_gate(c):
+            gate[c] = work.tile([P, GROUPS, CHUNK], F32, name="gate")
+            for pair in range(GROUPS // 2):
+                nc.scalar.activation(
+                    out=gate[c][:, 2 * pair : 2 * pair + 2, :], in_=g_ps[c, pair][:], func=ACT.Silu
+                )
+
+        def gamma_beta(c):
+            gb = weights["gb"]
+            zn[c] = work.tile([P, GROUPS, CHUNK], F32, name="zn")
+            for j in range(GROUPS):
+                nc.scalar.activation(
+                    out=zn[c][:, j, :],
+                    in_=zcT_ps[c, j // 2][:, j % 2, :],
+                    func=ACT.Identity,
+                    scale=gb[:, j : j + 1],
+                    bias=gb[:, GROUPS + j : GROUPS + j + 1],
+                )
+
+        def gated(c):
+            h_grouped[c] = work.tile([P, CHUNK * PACK], BF16, name="h_grouped", align_bytes=64)
+            nc.vector.tensor_tensor(
+                out=h_grouped[c][:].rearrange("p (w j) -> p w j", j=PACK),
+                in0=zn[c][:].rearrange("p j w -> p w j"),
+                in1=gate[c][:].rearrange("p j w -> p w j"),
+                op=ALU.mult,
+            )
+
+        def second_product(c):
+            wo_codes, wo_scales = weights["wo"]
+            h_codes, h_scales = h_mx[c]
+            for r in range(TILES):
+                out_ps[c, r] = psum.tile([P, H], F32, name="out_ps")
+                nc.tensor.matmul_mx(
+                    out=out_ps[c, r][:],
+                    lhsT=h_codes[:, r * P : (r + 1) * P].bitcast(FP8X4),
+                    lhsT_scale=h_scales[:, r * P : (r + 1) * P],
+                    rhs=wo_codes[:].bitcast(FP8X4),
+                    rhs_scale=wo_scales[:],
+                    start=True,
+                    stop=True,
+                )
+
+        def store(c):
+            out_sb = stores.tile([P, TILES * H], F32, name="out_sb")
+            for r in range(TILES):
+                nc.scalar.copy(out=out_sb[:, r * H : (r + 1) * H], in_=out_ps[c, r][:])
+            nc.sync.dma_start(out=out_chunks[c], in_=out_sb[:])
+
+        def live(c):
+            return 0 <= c < N_CHUNKS
+
+        def step(t):
+            if live(t + 2):
+                regroup_hs(t + 2)
+                centre_and_scale(t + 2, 0)
+            if live(t):
+                h_mx[t] = quantise(h_grouped[t], "h")
+            if live(t + 2):
+                centre_and_scale(t + 2, 1)
+                hs_mx[t + 2] = quantise(hs_grouped[t + 2], "hs")
+            if live(t + 1):
+                silu_gate(t + 1)
+            if live(t):
+                second_product(t)
+            if live(t + 2):
+                first_product(t + 2)
+            if live(t + 1):
+                gamma_beta(t + 1)
+            if live(t + 2):
+                transpose_zc(t + 2)
+            if live(t + 3):
+                transpose_hs(t + 3)
+            if live(t + 4):
+                token_statistics(t + 4)
+            if live(t):
+                store(t)
+            if live(t + 1):
+                gated(t + 1)
+
+        step(-4)
+        wg_grouped = regroup_weight(nc.vector.tensor_copy, wg_raw, "wg_grouped")
+        step(-3)
+        weights["wg"] = quantise_weight(wg_grouped, "wg")
+        wo_grouped = regroup_weight(nc.scalar.copy, wo_raw, "wo_grouped")
+        weights["gb"] = spread_gamma_beta()
+        step(-2)
+        weights["wo"] = quantise_weight(wo_grouped, "wo")
+        for t in range(-1, N_CHUNKS):
+            step(t)

@@ -20,6 +20,7 @@ CHUNK = TILES * P
 N_CHUNKS = TOKENS // CHUNK
 GROUPS = H // P
 HALVES = 2
+RUN = 4
 LN_EPS = 1e-5
 STORE_BUFS = 6
 
@@ -214,9 +215,9 @@ def tile_gatedlinearattention_pb_t_kernel(tc, z, hidden_states, Wg, Wo, gamma, b
         def gated(c):
             h_grouped[c] = work.tile([P, CHUNK * PACK], BF16, name="h_grouped", align_bytes=64)
             nc.vector.tensor_tensor(
-                out=h_grouped[c][:].rearrange("p (w j) -> p w j", j=PACK),
-                in0=zn[c][:].rearrange("p j w -> p w j"),
-                in1=gate[c][:].rearrange("p j w -> p w j"),
+                out=h_grouped[c][:].rearrange("p (a i j) -> p a j i", i=RUN, j=PACK),
+                in0=zn[c][:].rearrange("p j (a i) -> p a j i", i=RUN),
+                in1=gate[c][:].rearrange("p j (a i) -> p a j i", i=RUN),
                 op=ALU.mult,
             )
 

@@ -50,6 +50,8 @@ def tile_gatedlinearattention_pb_t_kernel(tc, z, hidden_states, Wg, Wo, gamma, b
         nc.scalar.activation(out=table_warmer[:], in_=minus_half[:, 0:1], func=ACT.Silu)
         gb_rows = const.tile([P, P], BF16, name="gb_rows")
         nc.vector.memset(gb_rows[:], 0.0)
+        nc.scalar.dma_start(out=gb_rows[0:GROUPS, :], in_=gamma.rearrange("(j p) -> j p", p=P))
+        nc.scalar.dma_start(out=gb_rows[GROUPS : 2 * GROUPS, :], in_=beta.rearrange("(j p) -> j p", p=P))
 
         z_sb = {}
         hs_sb = {}
@@ -70,14 +72,12 @@ def tile_gatedlinearattention_pb_t_kernel(tc, z, hidden_states, Wg, Wo, gamma, b
         )
         load_chunk(1)
         nc.sync.dma_start(out=wo_raw[:], in_=Wo.rearrange("(j p) n -> p j n", p=P))
-        nc.sync.dma_start(out=gb_rows[0:GROUPS, :], in_=gamma.rearrange("(j p) -> j p", p=P))
-        nc.sync.dma_start(out=gb_rows[GROUPS : 2 * GROUPS, :], in_=beta.rearrange("(j p) -> j p", p=P))
         for c in range(2, N_CHUNKS):
             load_chunk(c)
 
-        def regroup_weight(copy, raw, name):
+        def regroup_weight(raw, name):
             grouped = const.tile([P, H, PACK], BF16, name=name, align_bytes=64)
-            copy(out=grouped[:], in_=raw[:].rearrange("p t n -> p n t"))
+            nc.vector.tensor_copy(out=grouped[:], in_=raw[:].rearrange("p t n -> p n t"))
             return grouped
 
         def quantise_weight(grouped, name):
@@ -101,6 +101,7 @@ def tile_gatedlinearattention_pb_t_kernel(tc, z, hidden_states, Wg, Wo, gamma, b
 
         mean_var = {}
         rstd = {}
+        neg_mean = {}
         zc = {}
         zcT_ps = {}
         hsT_ps = {}
@@ -127,18 +128,22 @@ def tile_gatedlinearattention_pb_t_kernel(tc, z, hidden_states, Wg, Wo, gamma, b
             )
             rstd[c] = stats.tile([P, TILES], F32, name="rstd")
             nc.gpsimd.tensor_tensor(out=rstd[c][:], in0=var_eps[:], in1=minus_half[:], op=ALU.pow)
-
-        def centre_and_scale(c, r):
-            if r == 0:
-                zc[c] = work.tile([P, TILES, H], F32, name="zc")
-            nc.vector.tensor_scalar(
-                out=zc[c][:, r, :],
-                in0=z_sb[c][:, r * H : (r + 1) * H],
-                scalar1=mean_var[c][:, r, 0:1],
-                scalar2=rstd[c][:, r : r + 1],
-                op0=ALU.subtract,
-                op1=ALU.mult,
+            neg_mean[c] = stats.tile([P, TILES], F32, name="neg_mean")
+            nc.gpsimd.tensor_scalar(
+                out=neg_mean[c][:], in0=mean_var[c][:, :, 0], scalar1=-1.0, scalar2=None, op0=ALU.mult
             )
+
+        def centre_and_scale(c):
+            zc[c] = work.tile([P, TILES, H], F32, name="zc")
+            for r in range(TILES):
+                nc.gpsimd.tensor_scalar(
+                    out=zc[c][:, r, :],
+                    in0=z_sb[c][:, r * H : (r + 1) * H],
+                    scalar1=neg_mean[c][:, r : r + 1],
+                    scalar2=rstd[c][:, r : r + 1],
+                    op0=ALU.add,
+                    op1=ALU.mult,
+                )
 
         def transpose_zc(c):
             for pair in range(GROUPS // 2):
@@ -164,8 +169,7 @@ def tile_gatedlinearattention_pb_t_kernel(tc, z, hidden_states, Wg, Wo, gamma, b
 
         def regroup_hs(c):
             hs_grouped[c] = work.tile([P, CHUNK * PACK], BF16, name="hs_grouped", align_bytes=64)
-            copy = nc.vector.tensor_copy if c % 2 == 0 else nc.scalar.copy
-            copy(
+            nc.vector.tensor_copy(
                 out=hs_grouped[c][:].bitcast(F32).rearrange("p (w u) -> p w u", u=HALVES),
                 in_=hsT_ps[c][:].rearrange("p u w -> p w u"),
             )
@@ -247,13 +251,12 @@ def tile_gatedlinearattention_pb_t_kernel(tc, z, hidden_states, Wg, Wo, gamma, b
 
         def step(t):
             if live(t + 2):
-                regroup_hs(t + 2)
-                centre_and_scale(t + 2, 0)
+                hs_mx[t + 2] = quantise(hs_grouped[t + 2], "hs")
             if live(t):
                 h_mx[t] = quantise(h_grouped[t], "h")
-            if live(t + 2):
-                centre_and_scale(t + 2, 1)
-                hs_mx[t + 2] = quantise(hs_grouped[t + 2], "hs")
+            if live(t + 3):
+                regroup_hs(t + 3)
+                centre_and_scale(t + 3)
             if live(t + 1):
                 silu_gate(t + 1)
             if live(t):
@@ -264,9 +267,8 @@ def tile_gatedlinearattention_pb_t_kernel(tc, z, hidden_states, Wg, Wo, gamma, b
                 gamma_beta(t + 1)
             if live(t + 2):
                 transpose_zc(t + 2)
-            if live(t + 3):
-                transpose_hs(t + 3)
             if live(t + 4):
+                transpose_hs(t + 4)
                 token_statistics(t + 4)
             if live(t):
                 store(t)
@@ -274,12 +276,13 @@ def tile_gatedlinearattention_pb_t_kernel(tc, z, hidden_states, Wg, Wo, gamma, b
                 gated(t + 1)
 
         step(-4)
-        wg_grouped = regroup_weight(nc.vector.tensor_copy, wg_raw, "wg_grouped")
+        wg_grouped = regroup_weight(wg_raw, "wg_grouped")
         step(-3)
         weights["wg"] = quantise_weight(wg_grouped, "wg")
-        wo_grouped = regroup_weight(nc.scalar.copy, wo_raw, "wo_grouped")
         weights["gb"] = spread_gamma_beta()
         step(-2)
+        wo_grouped = regroup_weight(wo_raw, "wo_grouped")
+        step(-1)
         weights["wo"] = quantise_weight(wo_grouped, "wo")
-        for t in range(-1, N_CHUNKS):
+        for t in range(N_CHUNKS):
             step(t)

from contextlib import ExitStack

import concourse.mybir as mybir
from concourse.masks import make_identity

F32 = mybir.dt.float32
BF16 = mybir.dt.bfloat16
U32 = mybir.dt.uint32
U8 = mybir.dt.uint8
FP8X4 = mybir.dt.float8_e4m3fn_x4
ALU = mybir.AluOpType
ACT = mybir.ActivationFunctionType

P = 128
PACK = 4
H = 512
TOKENS = 16 * 256
TILES = 2
CHUNK = TILES * P
N_CHUNKS = TOKENS // CHUNK
GROUPS = H // P
HALVES = 2
RUN = 4
LN_EPS = 1e-5
STORE_BUFS = 6

FLOPS = 2 * 2 * TOKENS * H * H


def tile_gatedlinearattention_pb_t_kernel(tc, z, hidden_states, Wg, Wo, gamma, beta, out):
    nc = tc.nc

    z_chunks = z.flatten_outer_dims().rearrange("(c p r) f -> c p (r f)", p=P, r=TILES)
    hs_chunks = hidden_states.flatten_outer_dims().rearrange("(c p r) f -> c p (r f)", p=P, r=TILES)
    out_chunks = out.flatten_outer_dims().rearrange("(c p r) f -> c p (r f)", p=P, r=TILES)

    with ExitStack() as stack:
        const = stack.enter_context(tc.tile_pool(name="const", bufs=1))
        inputs = stack.enter_context(tc.tile_pool(name="inputs", bufs=N_CHUNKS))
        work = stack.enter_context(tc.tile_pool(name="work", bufs=3))
        stats = stack.enter_context(tc.tile_pool(name="stats", bufs=5))
        stores = stack.enter_context(tc.tile_pool(name="stores", bufs=STORE_BUFS))
        psum = stack.enter_context(tc.psum_pool(name="psum", bufs=2))

        ident = const.tile([P, P], F32, name="ident")
        make_identity(nc, ident[:])
        minus_half = const.tile([P, TILES], F32, name="minus_half")
        nc.gpsimd.memset(minus_half[:], -0.5)
        table_warmer = const.tile([P, 1], F32, name="table_warmer")
        nc.scalar.activation(out=table_warmer[:], in_=minus_half[:, 0:1], func=ACT.Silu)
        gb_rows = const.tile([P, P], BF16, name="gb_rows")
        nc.vector.memset(gb_rows[:], 0.0)
        nc.scalar.dma_start(out=gb_rows[0:GROUPS, :], in_=gamma.rearrange("(j p) -> j p", p=P))
        nc.scalar.dma_start(out=gb_rows[GROUPS : 2 * GROUPS, :], in_=beta.rearrange("(j p) -> j p", p=P))

        z_sb = {}
        hs_sb = {}

        def load_chunk(c):
            z_sb[c] = inputs.tile([P, TILES * H], BF16, name="z_sb")
            nc.sync.dma_start(out=z_sb[c][:], in_=z_chunks[c])
            hs_sb[c] = inputs.tile([P, TILES * H], BF16, name="hs_sb")
            nc.sync.dma_start(out=hs_sb[c][:], in_=hs_chunks[c])

        wg_raw = const.tile([P, PACK, H], BF16, name="wg_raw")
        wo_raw = const.tile([P, PACK, H], BF16, name="wo_raw")

        load_chunk(0)
        nc.sync.dma_start(
            out=wg_raw[:].rearrange("q (u e) n -> q u (e n)", u=HALVES),
            in_=Wg.rearrange("(u q e) n -> q u (e n)", u=HALVES, q=P),
        )
        load_chunk(1)
        nc.sync.dma_start(out=wo_raw[:], in_=Wo.rearrange("(j p) n -> p j n", p=P))
        for c in range(2, N_CHUNKS):
            load_chunk(c)

        def regroup_weight(raw, name):
            grouped = const.tile([P, H, PACK], BF16, name=name, align_bytes=64)
            nc.vector.tensor_copy(out=grouped[:], in_=raw[:].rearrange("p t n -> p n t"))
            return grouped

        def quantise_weight(grouped, name):
            codes = const.tile([P, H], U32, name=name + "_codes", align_bytes=64)
            scales = const.tile([P, H], U8, name=name + "_scales", align_bytes=64)
            nc.vector.quantize_mx(
                out=codes[:].bitcast(FP8X4),
                scales=scales[:],
                in_=grouped[:].rearrange("p n t -> p (n t)"),
            )
            return codes, scales

        def spread_gamma_beta():
            gb_rows_f32 = const.tile([P, P], F32, name="gb_rows_f32")
            nc.vector.tensor_copy(out=gb_rows_f32[:], in_=gb_rows[:])
            gb_ps = psum.tile([P, HALVES, CHUNK], F32, name="gb_ps", tag="hsT_ps")
            nc.tensor.transpose(gb_ps[:, 0, 0:P], gb_rows_f32[:], ident[:])
            gb = const.tile([P, 2 * GROUPS], F32, name="gb")
            nc.vector.tensor_copy(out=gb[:], in_=gb_ps[:, 0, 0 : 2 * GROUPS])
            return gb

        mean_var = {}
        rstd = {}
        neg_mean = {}
        zc = {}
        zcT_ps = {}
        hsT_ps = {}
        hs_grouped = {}
        hs_mx = {}
        g_ps = {}
        gate = {}
        zn = {}
        h_grouped = {}
        h_mx = {}
        out_ps = {}
        weights = {}

        def token_statistics(c):
            partial = stats.tile([P, TILES, 6], F32, name="partial")
            mean_var[c] = stats.tile([P, TILES, 2], F32, name="mean_var")
            for r in range(TILES):
                nc.vector.bn_stats(out=partial[:, r, :], in_=z_sb[c][:, r * H : (r + 1) * H])
            for r in range(TILES):
                nc.vector.bn_aggr(out=mean_var[c][:, r, :], in_=partial[:, r, :])
            var_eps = stats.tile([P, TILES], F32, name="var_eps")
            nc.gpsimd.tensor_scalar(
                out=var_eps[:], in0=mean_var[c][:, :, 1], scalar1=LN_EPS, scalar2=None, op0=ALU.add
            )
            rstd[c] = stats.tile([P, TILES], F32, name="rstd")
            nc.gpsimd.tensor_tensor(out=rstd[c][:], in0=var_eps[:], in1=minus_half[:], op=ALU.pow)
            neg_mean[c] = stats.tile([P, TILES], F32, name="neg_mean")
            nc.gpsimd.tensor_scalar(
                out=neg_mean[c][:], in0=mean_var[c][:, :, 0], scalar1=-1.0, scalar2=None, op0=ALU.mult
            )

        def centre_and_scale(c):
            zc[c] = work.tile([P, TILES, H], F32, name="zc")
            for r in range(TILES):
                nc.gpsimd.tensor_scalar(
                    out=zc[c][:, r, :],
                    in0=z_sb[c][:, r * H : (r + 1) * H],
                    scalar1=neg_mean[c][:, r : r + 1],
                    scalar2=rstd[c][:, r : r + 1],
                    op0=ALU.add,
                    op1=ALU.mult,
                )

        def transpose_zc(c):
            for pair in range(GROUPS // 2):
                zcT_ps[c, pair] = psum.tile([P, 2, CHUNK], F32, name="zcT_ps")
                for i in range(2):
                    j = 2 * pair + i
                    for r in range(TILES):
                        nc.tensor.transpose(
                            zcT_ps[c, pair][:, i, r * P : (r + 1) * P],
                            zc[c][:, r, j * P : (j + 1) * P],
                            ident[:],
                        )

        def transpose_hs(c):
            words = hs_sb[c][:].bitcast(F32)
            hsT_ps[c] = psum.tile([P, HALVES, CHUNK], F32, name="hsT_ps")
            for r in range(TILES):
                for u in range(HALVES):
                    first = (r * HALVES + u) * P
                    nc.tensor.transpose(
                        hsT_ps[c][:, u, r * P : (r + 1) * P], words[:, first : first + P], ident[:]
                    )

        def regroup_hs(c):
            hs_grouped[c] = work.tile([P, CHUNK * PACK], BF16, name="hs_grouped", align_bytes=64)
            nc.vector.tensor_copy(
                out=hs_grouped[c][:].bitcast(F32).rearrange("p (w u) -> p w u", u=HALVES),
                in_=hsT_ps[c][:].rearrange("p u w -> p w u"),
            )

        def quantise(grouped, name):
            codes = work.tile([P, CHUNK], U32, name=name + "_codes", align_bytes=64)
            scales = work.tile([P, CHUNK], U8, name=name + "_scales", align_bytes=64)
            nc.vector.quantize_mx(out=codes[:].bitcast(FP8X4), scales=scales[:], in_=grouped[:])
            return codes, scales

        def first_product(c):
            wg_codes, wg_scales = weights["wg"]
            hs_codes, hs_scales = hs_mx[c]
            for pair in range(GROUPS // 2):
                g_ps[c, pair] = psum.tile([P, 2, CHUNK], F32, name="g_ps")
                for i in range(2):
                    j = 2 * pair + i
                    nc.tensor.matmul_mx(
                        out=g_ps[c, pair][:, i, :],
                        lhsT=wg_codes[:, j * P : (j + 1) * P].bitcast(FP8X4),
                        lhsT_scale=wg_scales[:, j * P : (j + 1) * P],
                        rhs=hs_codes[:].bitcast(FP8X4),
                        rhs_scale=hs_scales[:],
                        start=True,
                        stop=True,
                    )

        def silu_gate(c):
            gate[c] = work.tile([P, GROUPS, CHUNK], F32, name="gate")
            for pair in range(GROUPS // 2):
                nc.scalar.activation(
                    out=gate[c][:, 2 * pair : 2 * pair + 2, :], in_=g_ps[c, pair][:], func=ACT.Silu
                )

        def gamma_beta(c):
            gb = weights["gb"]
            zn[c] = work.tile([P, GROUPS, CHUNK], F32, name="zn")
            for j in range(GROUPS):
                nc.scalar.activation(
                    out=zn[c][:, j, :],
                    in_=zcT_ps[c, j // 2][:, j % 2, :],
                    func=ACT.Identity,
                    scale=gb[:, j : j + 1],
                    bias=gb[:, GROUPS + j : GROUPS + j + 1],
                )

        def gated(c):
            h_grouped[c] = work.tile([P, CHUNK * PACK], BF16, name="h_grouped", align_bytes=64)
            nc.vector.tensor_tensor(
                out=h_grouped[c][:].rearrange("p (a i j) -> p a j i", i=RUN, j=PACK),
                in0=zn[c][:].rearrange("p j (a i) -> p a j i", i=RUN),
                in1=gate[c][:].rearrange("p j (a i) -> p a j i", i=RUN),
                op=ALU.mult,
            )

        def second_product(c):
            wo_codes, wo_scales = weights["wo"]
            h_codes, h_scales = h_mx[c]
            for r in range(TILES):
                out_ps[c, r] = psum.tile([P, H], F32, name="out_ps")
                nc.tensor.matmul_mx(
                    out=out_ps[c, r][:],
                    lhsT=h_codes[:, r * P : (r + 1) * P].bitcast(FP8X4),
                    lhsT_scale=h_scales[:, r * P : (r + 1) * P],
                    rhs=wo_codes[:].bitcast(FP8X4),
                    rhs_scale=wo_scales[:],
                    start=True,
                    stop=True,
                )

        def store(c):
            out_sb = stores.tile([P, TILES * H], F32, name="out_sb")
            for r in range(TILES):
                nc.scalar.copy(out=out_sb[:, r * H : (r + 1) * H], in_=out_ps[c, r][:])
            nc.sync.dma_start(out=out_chunks[c], in_=out_sb[:])

        def live(c):
            return 0 <= c < N_CHUNKS

        def step(t):
            if live(t + 2):
                hs_mx[t + 2] = quantise(hs_grouped[t + 2], "hs")
            if live(t):
                h_mx[t] = quantise(h_grouped[t], "h")
            if live(t + 3):
                regroup_hs(t + 3)
                centre_and_scale(t + 3)
            if live(t + 1):
                silu_gate(t + 1)
            if live(t):
                second_product(t)
            if live(t + 2):
                first_product(t + 2)
            if live(t + 1):
                gamma_beta(t + 1)
            if live(t + 2):
                transpose_zc(t + 2)
            if live(t + 4):
                transpose_hs(t + 4)
                token_statistics(t + 4)
            if live(t):
                store(t)
            if live(t + 1):
                gated(t + 1)

        step(-4)
        wg_grouped = regroup_weight(wg_raw, "wg_grouped")
        step(-3)
        weights["wg"] = quantise_weight(wg_grouped, "wg")
        weights["gb"] = spread_gamma_beta()
        step(-2)
        wo_grouped = regroup_weight(wo_raw, "wo_grouped")
        step(-1)
        weights["wo"] = quantise_weight(wo_grouped, "wo")
        for t in range(N_CHUNKS):
            step(t)
